import numpy as np
import ml_dtypes


def mxq(x, axis, fmt="e4m3"):
    dtype, down = {"e4m3": (ml_dtypes.float8_e4m3fn, 7), "e5m2": (ml_dtypes.float8_e5m2, 14)}[fmt]
    v = np.moveaxis(np.asarray(x, np.float32).astype(ml_dtypes.bfloat16).astype(np.float64), axis, -1)
    blocks = v.reshape(v.shape[:-1] + (-1, 32))
    amax = np.abs(blocks).max(-1, keepdims=True)
    byte = np.maximum(np.where(amax > 0, np.frexp(amax)[1] - 1 + 127, 0) - down, 1)
    scale = np.exp2(byte - 127.0)
    codes = (blocks / scale).astype(np.float32).astype(dtype).astype(np.float64)
    return np.moveaxis((codes * scale).reshape(v.shape), -1, axis)


WIDE = False


def mx_kscale(k):
    if not WIDE:
        return np.ones(k)
    levels = np.array([10, -10, 5, -5, 0])
    a = np.random.permutation(np.resize(levels, k // 512 * 4)).reshape(k // 512, 4)
    idx = np.arange(k)
    return np.exp2(a[idx // 512, idx % 128 // 32])


BF16 = ml_dtypes.bfloat16


def bf(x):
    return np.asarray(x, np.float32).astype(BF16)


def f64(x):
    return np.asarray(x).astype(np.float64)


L, H, SQ, SK, D, DV = 1, 4, 512, 512, 512, 512
SCALE = 1.0 / np.sqrt(D)


def setup_inputs():
    s = mx_kscale(D)
    return {"x1": bf(np.random.standard_normal(1)),
            "query": bf(np.random.standard_normal((L, H, SQ, D)) * 1.5 * s),
            "key": bf(np.random.standard_normal((L, H, SK, D)) / s),
            "value": bf(np.random.standard_normal((L, H, SK, DV)) * 0.18 * SQ / np.sqrt(SK))}


def reference(x1, query, key, value):
    qk = mxq(f64(query), 3, "e4m3") @ mxq(f64(key), 3, "e4m3").transpose(0, 1, 3, 2)
    scaled_qk = qk * SCALE
    e = np.exp(scaled_qk - scaled_qk.max(axis=2, keepdims=True))
    softmax_qk = e / e.sum(axis=2, keepdims=True)
    return mxq(softmax_qk, 3, "e4m3") @ mxq(f64(value), 2, "e4m3")

@@ -1,0 +1,215 @@
+import math
+from contextlib import ExitStack
+
+import concourse.mybir as mybir
+from concourse.masks import make_identity
+
+F32 = mybir.dt.float32
+BF16 = mybir.dt.bfloat16
+U32 = mybir.dt.uint32
+U8 = mybir.dt.uint8
+FP8X4 = mybir.dt.float8_e4m3fn_x4
+ACT = mybir.ActivationFunctionType
+ALU = mybir.AluOpType
+AX = mybir.AxisListType
+
+P = 128
+PACK = 4
+HEADS = 4
+N = 512
+SCALE = 1.0 / math.sqrt(N)
+FLOPS = 2 * 2 * HEADS * N * N * N
+
+PINNED = False
+
+
+def tile_model_kernel(tc, x1, query, key, value, out):
+    nc = tc.nc
+    with ExitStack() as ctx:
+        const = ctx.enter_context(tc.tile_pool(name="const", bufs=1))
+        raw = ctx.enter_context(tc.tile_pool(name="raw", bufs=HEADS))
+        grp = ctx.enter_context(tc.tile_pool(name="grp", bufs=2))
+        mxp = ctx.enter_context(tc.tile_pool(name="mxp", bufs=2))
+        soft = ctx.enter_context(tc.tile_pool(name="soft", bufs=2))
+        small = ctx.enter_context(tc.tile_pool(name="small", bufs=2))
+        res = ctx.enter_context(tc.tile_pool(name="res", bufs=2))
+        psum = ctx.enter_context(tc.psum_pool(name="psum", bufs=8))
+        if PINNED:
+            ctx.enter_context(tc.manual_schedule())
+
+        def bank(name):
+            return psum.tile([P, N], F32, name=name, tag="bank")
+
+        q_raw, k_raw, v_raw = [], [], []
+        for h in range(HEADS):
+            for lst, src, nm in ((q_raw, query, "q_raw"), (k_raw, key, "k_raw"), (v_raw, value, "v_raw")):
+                t = raw.tile([P, PACK, N], BF16, name=nm, tag=nm)
+                view = src[0, h].rearrange("(p j) d -> p j d", j=PACK)
+                if h == 0 and nm != "v_raw":
+                    nc.sync.dma_start(out=t[:, 0:2, :], in_=view[:, 0:2, :])
+                    nc.sync.dma_start(out=t[:, 2:4, :], in_=view[:, 2:4, :])
+                else:
+                    nc.sync.dma_start(out=t[:], in_=view)
+                lst.append(t)
+
+        ident = const.tile([P, P], F32, name="ident")
+        make_identity(nc, ident[:])
+        warm_in = const.tile([P, 1], F32, name="warm_in")
+        warm_out = const.tile([P, 1], F32, name="warm_out")
+        nc.vector.memset(warm_in[:], 0.0)
+        nc.scalar.activation(out=warm_out[:], in_=warm_in[:], func=ACT.Exp)
+
+        state = {}
+
+        def transposes(h):
+            banks = []
+            for x_raw, nm in ((q_raw[h], "tq"), (k_raw[h], "tk")):
+                words = x_raw[:].rearrange("p j d -> p (j d)").bitcast(F32)
+                for b in range(2):
+                    tp = bank(nm)
+                    tpv = tp[:].rearrange("p (u r) -> p u r", u=2)
+                    for jj in range(2):
+                        for u in range(2):
+                            j = 2 * b + jj
+                            c0 = (N // 2) * j + P * u
+                            nc.tensor.transpose(tpv[:, u, P * jj : P * jj + P], words[:, c0 : c0 + P], ident[:])
+                    banks.append(tpv)
+            state[("tp", h)] = banks
+
+        def gather(h, engines):
+            banks = state[("tp", h)]
+            qg = grp.tile([P, N * PACK], BF16, name="qg", tag="qg", align_bytes=64)
+            kg = grp.tile([P, N * PACK], BF16, name="kg", tag="kg", align_bytes=64)
+            for i, (xg, b) in enumerate(((qg, 0), (qg, 1), (kg, 0), (kg, 1))):
+                dst = xg[:].bitcast(F32)[:, N * b : N * b + N].rearrange("p (r u) -> p r u", u=2)
+                srcv = banks[i].rearrange("p u r -> p r u")
+                if engines[i] == "s":
+                    nc.scalar.copy(out=dst, in_=srcv)
+                else:
+                    nc.vector.tensor_copy(out=dst, in_=srcv)
+            state[("qg", h)] = qg
+            state[("kg", h)] = kg
+
+        def quantise(h, what):
+            codes = mxp.tile([P, N], U32, name=what + "_codes", tag=what + "_codes", align_bytes=64)
+            scales = mxp.tile([P, N], U8, name=what + "_scales", tag=what + "_scales", align_bytes=64)
+            nc.vector.quantize_mx(out=codes[:].bitcast(FP8X4), scales=scales[:], in_=state[(what + "g", h)][:])
+            state[(what, h)] = (codes, scales)
+
+        def scores(h):
+            kc, ks = state[("k", h)]
+            qc, qs = state[("q", h)]
+            sts = []
+            for t in range(PACK):
+                st = bank("st")
+                cols = slice(P * t, P * t + P)
+                nc.tensor.matmul_mx(
+                    out=st[:],
+                    lhsT=kc[:, cols].bitcast(FP8X4),
+                    lhsT_scale=ks[:, cols],
+                    rhs=qc[:].bitcast(FP8X4),
+                    rhs_scale=qs[:],
+                    start=True,
+                    stop=True,
+                )
+                sts.append(st)
+            state[("st", h)] = sts
+
+        def softmax_exp(h):
+            sts = state[("st", h)]
+            mx = small.tile([P, PACK], F32, name="mx", tag="mx")
+            nb = small.tile([P, PACK], F32, name="nb", tag="nb")
+            sums = small.tile([P, PACK], F32, name="sums", tag="sums")
+            e = soft.tile([P, PACK, N], F32, name="e", tag="e")
+            for t in range(PACK):
+                nc.vector.reduce_max(out=mx[:, t : t + 1], in_=sts[t][:], axis=AX.X)
+                nc.scalar.mul(out=nb[:, t : t + 1], in_=mx[:, t : t + 1], mul=-SCALE)
+                nc.scalar.activation(
+                    out=e[:, t, :],
+                    in_=sts[t][:],
+                    func=ACT.Exp,
+                    bias=nb[:, t : t + 1],
+                    scale=SCALE,
+                    accum_out=sums[:, t : t + 1],
+                )
+            state[("e", h)] = (e, sums)
+
+        def regroup_v(h):
+            vg = grp.tile([P, N * PACK], BF16, name="vg", tag="vg", align_bytes=64)
+            nc.vector.tensor_copy(
+                out=vg[:].rearrange("p (c i t) -> p c t i", i=4, t=PACK),
+                in_=v_raw[h][:].rearrange("p t (c i) -> p c t i", i=4),
+            )
+            state[("vg", h)] = vg
+
+        def normalise(h):
+            e, sums = state[("e", h)]
+            r = small.tile([P, PACK], F32, name="r", tag="r")
+            nc.vector.reciprocal(out=r[:], in_=sums[:])
+            pg = grp.tile([P, N * PACK], BF16, name="pg", tag="pg", align_bytes=64)
+            nc.vector.tensor_tensor(
+                out=pg[:].rearrange("p (c t) -> p c t", t=PACK),
+                in0=e[:].rearrange("p t c -> p c t"),
+                in1=r[:].unsqueeze(1).to_broadcast([P, N, PACK]),
+                op=ALU.mult,
+            )
+            state[("pg", h)] = pg
+
+        def weighted_sum(h):
+            pc, ps = state[("p", h)]
+            vc, vs = state[("v", h)]
+            ots = []
+            for j in range(PACK):
+                ot = bank("ot")
+                cols = slice(P * j, P * j + P)
+                nc.tensor.matmul_mx(
+                    out=ot[:],
+                    lhsT=pc[:, cols].bitcast(FP8X4),
+                    lhsT_scale=ps[:, cols],
+                    rhs=vc[:].bitcast(FP8X4),
+                    rhs_scale=vs[:],
+                    start=True,
+                    stop=True,
+                )
+                ots.append(ot)
+            state[("ot", h)] = ots
+
+        def store(h, engines, per_store):
+            ots = state[("ot", h)]
+            o_sb = res.tile([P, PACK, N], F32, name="o_sb", tag="o_sb")
+            view = out[0, h].rearrange("(p j) n -> p j n", j=PACK)
+            for j in range(PACK):
+                if engines[j] == "s":
+                    nc.scalar.copy(out=o_sb[:, j, :], in_=ots[j][:])
+                else:
+                    nc.vector.tensor_copy(out=o_sb[:, j, :], in_=ots[j][:])
+                if (j + 1) % per_store == 0:
+                    js = slice(j + 1 - per_store, j + 1)
+                    nc.sync.dma_start(out=view[:, js, :], in_=o_sb[:, js, :])
+
+        transposes(0)
+        gather(0, "svsv")
+        quantise(0, "q")
+        quantise(0, "k")
+        scores(0)
+
+        for h in range(HEADS):
+            if h > 0:
+                weighted_sum(h - 1)
+            softmax_exp(h)
+            regroup_v(h)
+            if h + 1 < HEADS:
+                transposes(h + 1)
+                gather(h + 1, "ssss")
+            if h > 0:
+                store(h - 1, "ssss", 2)
+            normalise(h)
+            quantise(h, "v")
+            if h + 1 < HEADS:
+                quantise(h + 1, "q")
+                quantise(h + 1, "k")
+            quantise(h, "p")
+            if h + 1 < HEADS:
+                scores(h + 1)
+        weighted_sum(HEADS - 1)
+        store(HEADS - 1, "svsv", 1)

@@ -20,7 +20,7 @@ N = 512
 SCALE = 1.0 / math.sqrt(N)
 FLOPS = 2 * 2 * HEADS * N * N * N
 
-PINNED = False
+PINNED = True
 
 
 def tile_model_kernel(tc, x1, query, key, value, out):

@@ -11,16 +11,14 @@ U8 = mybir.dt.uint8
 FP8X4 = mybir.dt.float8_e4m3fn_x4
 ACT = mybir.ActivationFunctionType
 ALU = mybir.AluOpType
-AX = mybir.AxisListType
 
 P = 128
 PACK = 4
+RUN = 4
 HEADS = 4
 N = 512
 SCALE = 1.0 / math.sqrt(N)
 FLOPS = 2 * 2 * HEADS * N * N * N
-
-PINNED = True
 
 
 def tile_model_kernel(tc, x1, query, key, value, out):
@@ -28,29 +26,35 @@ def tile_model_kernel(tc, x1, query, key, value, out):
     with ExitStack() as ctx:
         const = ctx.enter_context(tc.tile_pool(name="const", bufs=1))
         raw = ctx.enter_context(tc.tile_pool(name="raw", bufs=HEADS))
+        vgrp = ctx.enter_context(tc.tile_pool(name="vgrp", bufs=HEADS))
         grp = ctx.enter_context(tc.tile_pool(name="grp", bufs=2))
         mxp = ctx.enter_context(tc.tile_pool(name="mxp", bufs=2))
         soft = ctx.enter_context(tc.tile_pool(name="soft", bufs=2))
         small = ctx.enter_context(tc.tile_pool(name="small", bufs=2))
         res = ctx.enter_context(tc.tile_pool(name="res", bufs=2))
-        psum = ctx.enter_context(tc.psum_pool(name="psum", bufs=8))
-        if PINNED:
-            ctx.enter_context(tc.manual_schedule())
+        psum = ctx.enter_context(tc.psum_pool(name="psum", bufs=4))
+        ctx.enter_context(tc.manual_schedule())
 
-        def bank(name):
-            return psum.tile([P, N], F32, name=name, tag="bank")
+        def bank(name, half):
+            return psum.tile([P, N], F32, name=name, tag=half)
 
-        q_raw, k_raw, v_raw = [], [], []
-        for h in range(HEADS):
-            for lst, src, nm in ((q_raw, query, "q_raw"), (k_raw, key, "k_raw"), (v_raw, value, "v_raw")):
-                t = raw.tile([P, PACK, N], BF16, name=nm, tag=nm)
-                view = src[0, h].rearrange("(p j) d -> p j d", j=PACK)
-                if h == 0 and nm != "v_raw":
-                    nc.sync.dma_start(out=t[:, 0:2, :], in_=view[:, 0:2, :])
-                    nc.sync.dma_start(out=t[:, 2:4, :], in_=view[:, 2:4, :])
-                else:
-                    nc.sync.dma_start(out=t[:], in_=view)
-                lst.append(t)
+        raws = {}
+
+        def load(src, nm, h, pieces):
+            t = raw.tile([P, PACK, N], BF16, name=nm, tag=nm)
+            view = src[0, h].rearrange("(p j) d -> p j d", j=PACK)
+            step = PACK // pieces
+            for i in range(pieces):
+                js = slice(step * i, step * i + step)
+                nc.sync.dma_start(out=t[:, js, :], in_=view[:, js, :])
+            raws[(nm, h)] = t
+
+        for h in range(HEADS + 1):
+            if h < HEADS:
+                load(query, "q", h, 2 if h == 0 else 1)
+                load(key, "k", h, 2 if h == 0 else 1)
+            if h >= 1:
+                load(value, "v", h - 1, 1)
 
         ident = const.tile([P, P], F32, name="ident")
         make_identity(nc, ident[:])
@@ -61,34 +65,31 @@ def tile_model_kernel(tc, x1, query, key, value, out):
 
         state = {}
 
-        def transposes(h):
+        def transposes(h, half):
             banks = []
-            for x_raw, nm in ((q_raw[h], "tq"), (k_raw[h], "tk")):
-                words = x_raw[:].rearrange("p j d -> p (j d)").bitcast(F32)
+            for nm in ("q", "k"):
+                words = raws[(nm, h)][:].rearrange("p j d -> p (j d)").bitcast(F32)
                 for b in range(2):
-                    tp = bank(nm)
+                    tp = bank("t" + nm, half)
                     tpv = tp[:].rearrange("p (u r) -> p u r", u=2)
                     for jj in range(2):
                         for u in range(2):
-                            j = 2 * b + jj
-                            c0 = (N // 2) * j + P * u
+                            c0 = (N // 2) * (2 * b + jj) + P * u
                             nc.tensor.transpose(tpv[:, u, P * jj : P * jj + P], words[:, c0 : c0 + P], ident[:])
                     banks.append(tpv)
             state[("tp", h)] = banks
+            state[("qg", h)] = grp.tile([P, N * PACK], BF16, name="qg", tag="qg", align_bytes=64)
+            state[("kg", h)] = grp.tile([P, N * PACK], BF16, name="kg", tag="kg", align_bytes=64)
 
-        def gather(h, engines):
-            banks = state[("tp", h)]
-            qg = grp.tile([P, N * PACK], BF16, name="qg", tag="qg", align_bytes=64)
-            kg = grp.tile([P, N * PACK], BF16, name="kg", tag="kg", align_bytes=64)
-            for i, (xg, b) in enumerate(((qg, 0), (qg, 1), (kg, 0), (kg, 1))):
-                dst = xg[:].bitcast(F32)[:, N * b : N * b + N].rearrange("p (r u) -> p r u", u=2)
-                srcv = banks[i].rearrange("p u r -> p r u")
-                if engines[i] == "s":
-                    nc.scalar.copy(out=dst, in_=srcv)
-                else:
-                    nc.vector.tensor_copy(out=dst, in_=srcv)
-            state[("qg", h)] = qg
-            state[("kg", h)] = kg
+        def gather(h, i, engine):
+            xg = state[(("qg", "kg")[i // 2], h)]
+            b = i % 2
+            dst = xg[:].bitcast(F32)[:, N * b : N * b + N].rearrange("p (r u) -> p r u", u=2)
+            srcv = state[("tp", h)][i].rearrange("p u r -> p r u")
+            if engine == "s":
+                nc.scalar.copy(out=dst, in_=srcv)
+            else:
+                nc.vector.tensor_copy(out=dst, in_=srcv)
 
         def quantise(h, what):
             codes = mxp.tile([P, N], U32, name=what + "_codes", tag=what + "_codes", align_bytes=64)
@@ -96,83 +97,80 @@ def tile_model_kernel(tc, x1, query, key, value, out):
             nc.vector.quantize_mx(out=codes[:].bitcast(FP8X4), scales=scales[:], in_=state[(what + "g", h)][:])
             state[(what, h)] = (codes, scales)
 
-        def scores(h):
-            kc, ks = state[("k", h)]
-            qc, qs = state[("q", h)]
-            sts = []
+        def mx_passes(h, stat, mov, name, half):
+            sc, ss = state[(stat, h)]
+            mc, ms = state[(mov, h)]
+            tiles = []
             for t in range(PACK):
-                st = bank("st")
+                acc = bank(name, half)
                 cols = slice(P * t, P * t + P)
                 nc.tensor.matmul_mx(
-                    out=st[:],
-                    lhsT=kc[:, cols].bitcast(FP8X4),
-                    lhsT_scale=ks[:, cols],
-                    rhs=qc[:].bitcast(FP8X4),
-                    rhs_scale=qs[:],
+                    out=acc[:],
+                    lhsT=sc[:, cols].bitcast(FP8X4),
+                    lhsT_scale=ss[:, cols],
+                    rhs=mc[:].bitcast(FP8X4),
+                    rhs_scale=ms[:],
                     start=True,
                     stop=True,
                 )
-                sts.append(st)
-            state[("st", h)] = sts
+                tiles.append(acc)
+            state[(name, h)] = tiles
 
-        def softmax_exp(h):
+        def reciprocal(h):
+            r = small.tile([P, PACK], F32, name="r", tag="r")
+            nc.vector.reciprocal(out=r[:], in_=state[("sums", h)][:])
+            state[("r", h)] = r
+
+        def softmax_exp(h, gathered):
             sts = state[("st", h)]
-            mx = small.tile([P, PACK], F32, name="mx", tag="mx")
             nb = small.tile([P, PACK], F32, name="nb", tag="nb")
             sums = small.tile([P, PACK], F32, name="sums", tag="sums")
+            neg = soft.tile([P, PACK, N], F32, name="neg", tag="neg")
             e = soft.tile([P, PACK, N], F32, name="e", tag="e")
+            state[("sums", h)] = sums
+            state[("e", h)] = e
             for t in range(PACK):
-                nc.vector.reduce_max(out=mx[:, t : t + 1], in_=sts[t][:], axis=AX.X)
-                nc.scalar.mul(out=nb[:, t : t + 1], in_=mx[:, t : t + 1], mul=-SCALE)
+                if t == PACK - 1 and h >= 1:
+                    reciprocal(h - 1)
+                nc.vector.tensor_scalar(
+                    out=neg[:, t, :],
+                    in0=sts[t][:],
+                    scalar1=-SCALE,
+                    scalar2=None,
+                    op0=ALU.mult,
+                    op1=ALU.min,
+                    accum_out=nb[:, t : t + 1],
+                )
                 nc.scalar.activation(
                     out=e[:, t, :],
-                    in_=sts[t][:],
+                    in_=neg[:, t, :],
                     func=ACT.Exp,
                     bias=nb[:, t : t + 1],
-                    scale=SCALE,
+                    scale=-1.0,
                     accum_out=sums[:, t : t + 1],
                 )
-            state[("e", h)] = (e, sums)
+                if gathered < HEADS:
+                    gather(gathered, t, "s")
 
-        def regroup_v(h):
-            vg = grp.tile([P, N * PACK], BF16, name="vg", tag="vg", align_bytes=64)
-            nc.vector.tensor_copy(
-                out=vg[:].rearrange("p (c i t) -> p c t i", i=4, t=PACK),
-                in_=v_raw[h][:].rearrange("p t (c i) -> p c t i", i=4),
-            )
+        def regroup_v(h, engine):
+            vg = vgrp.tile([P, N * PACK], BF16, name="vg", tag="vg", align_bytes=64)
+            dst = vg[:].rearrange("p (c i t) -> p c t i", i=RUN, t=PACK)
+            srcv = raws[("v", h)][:].rearrange("p t (c i) -> p c t i", i=RUN)
+            if engine == "s":
+                nc.scalar.copy(out=dst, in_=srcv)
+            else:
+                nc.vector.tensor_copy(out=dst, in_=srcv)
             state[("vg", h)] = vg
 
         def normalise(h):
-            e, sums = state[("e", h)]
-            r = small.tile([P, PACK], F32, name="r", tag="r")
-            nc.vector.reciprocal(out=r[:], in_=sums[:])
             pg = grp.tile([P, N * PACK], BF16, name="pg", tag="pg", align_bytes=64)
             nc.vector.tensor_tensor(
-                out=pg[:].rearrange("p (c t) -> p c t", t=PACK),
-                in0=e[:].rearrange("p t c -> p c t"),
-                in1=r[:].unsqueeze(1).to_broadcast([P, N, PACK]),
+                out=pg[:].rearrange("p (c i t) -> p c t i", i=RUN, t=PACK),
+                in0=state[("e", h)][:].rearrange("p t (c i) -> p c t i", i=RUN),
+                in1=state[("r", h)][:].unsqueeze(1).unsqueeze(3).to_broadcast([P, N // RUN, PACK, RUN]),
                 op=ALU.mult,
             )
             state[("pg", h)] = pg
-
-        def weighted_sum(h):
-            pc, ps = state[("p", h)]
-            vc, vs = state[("v", h)]
-            ots = []
-            for j in range(PACK):
-                ot = bank("ot")
-                cols = slice(P * j, P * j + P)
-                nc.tensor.matmul_mx(
-                    out=ot[:],
-                    lhsT=pc[:, cols].bitcast(FP8X4),
-                    lhsT_scale=ps[:, cols],
-                    rhs=vc[:].bitcast(FP8X4),
-                    rhs_scale=vs[:],
-                    start=True,
-                    stop=True,
-                )
-                ots.append(ot)
-            state[("ot", h)] = ots
 
         def store(h, engines, per_store):
             ots = state[("ot", h)]
@@ -187,29 +185,38 @@ def tile_model_kernel(tc, x1, query, key, value, out):
                     js = slice(j + 1 - per_store, j + 1)
                     nc.sync.dma_start(out=view[:, js, :], in_=o_sb[:, js, :])
 
-        transposes(0)
-        gather(0, "svsv")
+        transposes(0, "A")
+        transposes(1, "B")
+        for i in range(4):
+            gather(0, i, "sv"[i % 2])
         quantise(0, "q")
         quantise(0, "k")
-        scores(0)
+        mx_passes(0, "k", "q", "st", "A")
+        for i in range(4):
+            gather(1, i, "s")
 
-        for h in range(HEADS):
-            if h > 0:
-                weighted_sum(h - 1)
-            softmax_exp(h)
-            regroup_v(h)
-            if h + 1 < HEADS:
-                transposes(h + 1)
-                gather(h + 1, "ssss")
-            if h > 0:
-                store(h - 1, "ssss", 2)
-            normalise(h)
-            quantise(h, "v")
-            if h + 1 < HEADS:
-                quantise(h + 1, "q")
-                quantise(h + 1, "k")
-            quantise(h, "p")
-            if h + 1 < HEADS:
-                scores(h + 1)
-        weighted_sum(HEADS - 1)
-        store(HEADS - 1, "svsv", 1)
+        for p in range(HEADS + 2):
+            if p >= 2:
+                mx_passes(p - 2, "p", "v", "ot", "B")
+            if p + 2 < HEADS:
+                transposes(p + 2, "B")
+            if p < HEADS:
+                softmax_exp(p, p + 2)
+            if p >= 2:
+                if p - 2 == HEADS - 1:
+                    store(p - 2, "svsv", 1)
+                else:
+                    store(p - 2, "ssss", 2)
+            if p + 1 < HEADS:
+                regroup_v(p + 1, "s")
+                quantise(p + 1, "q")
+                quantise(p + 1, "k")
+                mx_passes(p + 1, "k", "q", "st", "A")
+            if p == 0:
+                regroup_v(0, "v")
+            if 1 <= p <= HEADS:
+                if p == HEADS:
+                    reciprocal(p - 1)
+                normalise(p - 1)
+                quantise(p - 1, "v")
+                quantise(p - 1, "p")

@@ -19,6 +19,7 @@ HEADS = 4
 N = 512
 SCALE = 1.0 / math.sqrt(N)
 FLOPS = 2 * 2 * HEADS * N * N * N
+V_SHARE = (N // RUN, 0, 0, 0)
 
 
 def tile_model_kernel(tc, x1, query, key, value, out):
@@ -65,6 +66,12 @@ def tile_model_kernel(tc, x1, query, key, value, out):
 
         state = {}
 
+        def copy(engine, dst, srcv):
+            if engine == "s":
+                nc.scalar.copy(out=dst, in_=srcv)
+            else:
+                nc.vector.tensor_copy(out=dst, in_=srcv)
+
         def transposes(h, half):
             banks = []
             for nm in ("q", "k"):
@@ -85,36 +92,38 @@ def tile_model_kernel(tc, x1, query, key, value, out):
             xg = state[(("qg", "kg")[i // 2], h)]
             b = i % 2
             dst = xg[:].bitcast(F32)[:, N * b : N * b + N].rearrange("p (r u) -> p r u", u=2)
-            srcv = state[("tp", h)][i].rearrange("p u r -> p r u")
-            if engine == "s":
-                nc.scalar.copy(out=dst, in_=srcv)
-            else:
-                nc.vector.tensor_copy(out=dst, in_=srcv)
+            copy(engine, dst, state[("tp", h)][i].rearrange("p u r -> p r u"))
 
-        def quantise(h, what):
+        def mx_tiles(h, what):
             codes = mxp.tile([P, N], U32, name=what + "_codes", tag=what + "_codes", align_bytes=64)
             scales = mxp.tile([P, N], U8, name=what + "_scales", tag=what + "_scales", align_bytes=64)
-            nc.vector.quantize_mx(out=codes[:].bitcast(FP8X4), scales=scales[:], in_=state[(what + "g", h)][:])
             state[(what, h)] = (codes, scales)
 
-        def mx_passes(h, stat, mov, name, half):
+        def quantise(h, what, lo=0, hi=N):
+            if lo == 0:
+                mx_tiles(h, what)
+            codes, scales = state[(what, h)]
+            nc.vector.quantize_mx(
+                out=codes[:, lo:hi].bitcast(FP8X4),
+                scales=scales[:, lo:hi],
+                in_=state[(what + "g", h)][:, PACK * lo : PACK * hi],
+            )
+
+        def mx_pass(h, stat, mov, name, half, t):
             sc, ss = state[(stat, h)]
             mc, ms = state[(mov, h)]
-            tiles = []
-            for t in range(PACK):
-                acc = bank(name, half)
-                cols = slice(P * t, P * t + P)
-                nc.tensor.matmul_mx(
-                    out=acc[:],
-                    lhsT=sc[:, cols].bitcast(FP8X4),
-                    lhsT_scale=ss[:, cols],
-                    rhs=mc[:].bitcast(FP8X4),
-                    rhs_scale=ms[:],
-                    start=True,
-                    stop=True,
-                )
-                tiles.append(acc)
-            state[(name, h)] = tiles
+            acc = bank(name, half)
+            cols = slice(P * t, P * t + P)
+            nc.tensor.matmul_mx(
+                out=acc[:],
+                lhsT=sc[:, cols].bitcast(FP8X4),
+                lhsT_scale=ss[:, cols],
+                rhs=mc[:].bitcast(FP8X4),
+                rhs_scale=ms[:],
+                start=True,
+                stop=True,
+            )
+            state[(name, h, t)] = acc
 
         def reciprocal(h):
             r = small.tile([P, PACK], F32, name="r", tag="r")
@@ -122,7 +131,6 @@ def tile_model_kernel(tc, x1, query, key, value, out):
             state[("r", h)] = r
 
         def softmax_exp(h, gathered):
-            sts = state[("st", h)]
             nb = small.tile([P, PACK], F32, name="nb", tag="nb")
             sums = small.tile([P, PACK], F32, name="sums", tag="sums")
             neg = soft.tile([P, PACK, N], F32, name="neg", tag="neg")
@@ -134,7 +142,7 @@ def tile_model_kernel(tc, x1, query, key, value, out):
                     reciprocal(h - 1)
                 nc.vector.tensor_scalar(
                     out=neg[:, t, :],
-                    in0=sts[t][:],
+                    in0=state[("st", h, t)][:],
                     scalar1=-SCALE,
                     scalar2=None,
                     op0=ALU.mult,
@@ -153,34 +161,46 @@ def tile_model_kernel(tc, x1, query, key, value, out):
                     gather(gathered, t, "s")
 
         def regroup_v(h, engine):
-            vg = vgrp.tile([P, N * PACK], BF16, name="vg", tag="vg", align_bytes=64)
-            dst = vg[:].rearrange("p (c i t) -> p c t i", i=RUN, t=PACK)
+            if ("vg", h) not in state:
+                state[("vg", h)] = vgrp.tile([P, N * PACK], BF16, name="vg", tag="vg", align_bytes=64)
+            dst = state[("vg", h)][:].rearrange("p (c i t) -> p c t i", i=RUN, t=PACK)
             srcv = raws[("v", h)][:].rearrange("p t (c i) -> p c t i", i=RUN)
-            if engine == "s":
-                nc.scalar.copy(out=dst, in_=srcv)
-            else:
-                nc.vector.tensor_copy(out=dst, in_=srcv)
-            state[("vg", h)] = vg
+            cut = V_SHARE[h]
+            if engine == "v" and cut > 0:
+                copy("v", dst[:, 0:cut], srcv[:, 0:cut])
+            if engine == "s" and cut < N // RUN:
+                copy("s", dst[:, cut:], srcv[:, cut:])
 
-        def normalise(h):
-            pg = grp.tile([P, N * PACK], BF16, name="pg", tag="pg", align_bytes=64)
+        def normalise(h, lo, hi):
+            if lo == 0:
+                state[("pg", h)] = grp.tile([P, N * PACK], BF16, name="pg", tag="pg", align_bytes=64)
+            pg = state[("pg", h)]
             nc.vector.tensor_tensor(
-                out=pg[:].rearrange("p (c i t) -> p c t i", i=RUN, t=PACK),
-                in0=state[("e", h)][:].rearrange("p t (c i) -> p c t i", i=RUN),
-                in1=state[("r", h)][:].unsqueeze(1).unsqueeze(3).to_broadcast([P, N // RUN, PACK, RUN]),
+                out=pg[:, PACK * lo : PACK * hi].rearrange("p (c i t) -> p c t i", i=RUN, t=PACK),
+                in0=state[("e", h)][:, :, lo:hi].rearrange("p t (c i) -> p c t i", i=RUN),
+                in1=state[("r", h)][:].unsqueeze(1).unsqueeze(3).to_broadcast([P, (hi - lo) // RUN, PACK, RUN]),
                 op=ALU.mult,
             )
-            state[("pg", h)] = pg
+
+        def finish(h, chunks):
+            width = N // chunks
+            for i in range(chunks + 1):
+                if i < chunks:
+                    normalise(h, width * i, width * i + width)
+                if i == 0:
+                    quantise(h, "v")
+                    if h + 1 == HEADS - 1:
+                        reciprocal(h + 1)
+                if i >= 1:
+                    quantise(h, "p", width * (i - 1), width * i)
+                    for t in range(width * (i - 1) // P, width * i // P):
+                        mx_pass(h, "p", "v", "ot", "B", t)
 
         def store(h, engines, per_store):
-            ots = state[("ot", h)]
             o_sb = res.tile([P, PACK, N], F32, name="o_sb", tag="o_sb")
             view = out[0, h].rearrange("(p j) n -> p j n", j=PACK)
             for j in range(PACK):
-                if engines[j] == "s":
-                    nc.scalar.copy(out=o_sb[:, j, :], in_=ots[j][:])
-                else:
-                    nc.vector.tensor_copy(out=o_sb[:, j, :], in_=ots[j][:])
+                copy(engines[j], o_sb[:, j, :], state[("ot", h, j)][:])
                 if (j + 1) % per_store == 0:
                     js = slice(j + 1 - per_store, j + 1)
                     nc.sync.dma_start(out=view[:, js, :], in_=o_sb[:, js, :])
@@ -191,32 +211,29 @@ def tile_model_kernel(tc, x1, query, key, value, out):
             gather(0, i, "sv"[i % 2])
         quantise(0, "q")
         quantise(0, "k")
-        mx_passes(0, "k", "q", "st", "A")
+        for t in range(PACK):
+            mx_pass(0, "k", "q", "st", "A", t)
         for i in range(4):
             gather(1, i, "s")
 
         for p in range(HEADS + 2):
-            if p >= 2:
-                mx_passes(p - 2, "p", "v", "ot", "B")
             if p + 2 < HEADS:
                 transposes(p + 2, "B")
+            if p + 1 < HEADS:
+                quantise(p + 1, "q")
             if p < HEADS:
                 softmax_exp(p, p + 2)
             if p >= 2:
                 if p - 2 == HEADS - 1:
-                    store(p - 2, "svsv", 1)
+                    store(p - 2, "sssv", 1)
                 else:
                     store(p - 2, "ssss", 2)
             if p + 1 < HEADS:
                 regroup_v(p + 1, "s")
-                quantise(p + 1, "q")
                 quantise(p + 1, "k")
-                mx_passes(p + 1, "k", "q", "st", "A")
+                for t in range(PACK):
+                    mx_pass(p + 1, "k", "q", "st", "A", t)
             if p == 0:
                 regroup_v(0, "v")
             if 1 <= p <= HEADS:
-                if p == HEADS:
-                    reciprocal(p - 1)
-                normalise(p - 1)
-                quantise(p - 1, "v")
-                quantise(p - 1, "p")
+                finish(p - 1, PACK if p == HEADS else 1)

@@ -64,6 +64,9 @@ def tile_model_kernel(tc, x1, query, key, value, out):
         nc.vector.memset(warm_in[:], 0.0)
         nc.scalar.activation(out=warm_out[:], in_=warm_in[:], func=ACT.Exp)
 
+        zeros = const.tile([P, N], BF16, name="zeros")
+        nc.vector.memset(zeros[:], 0.0)
+
         state = {}
 
         def copy(engine, dst, srcv):
@@ -72,13 +75,15 @@ def tile_model_kernel(tc, x1, query, key, value, out):
             else:
                 nc.vector.tensor_copy(out=dst, in_=srcv)
 
-        def transposes(h, half):
+        def transposes(h, half, warm=(0, 0, 0, 0)):
             banks = []
             for nm in ("q", "k"):
                 words = raws[(nm, h)][:].rearrange("p j d -> p (j d)").bitcast(F32)
                 for b in range(2):
                     tp = bank("t" + nm, half)
                     tpv = tp[:].rearrange("p (u r) -> p u r", u=2)
+                    for w in range(warm[len(banks)]):
+                        nc.tensor.matmul(out=tp[:], lhsT=zeros[:, 0:P], rhs=zeros[:], start=True, stop=True)
                     for jj in range(2):
                         for u in range(2):
                             c0 = (N // 2) * (2 * b + jj) + P * u
@@ -205,8 +210,8 @@ def tile_model_kernel(tc, x1, query, key, value, out):
                     js = slice(j + 1 - per_store, j + 1)
                     nc.sync.dma_start(out=view[:, js, :], in_=o_sb[:, js, :])
 
-        transposes(0, "A")
-        transposes(1, "B")
+        transposes(0, "A", (3, 1, 1, 1))
+        transposes(1, "B", (1, 1, 1, 0))
         for i in range(4):
             gather(0, i, "sv"[i % 2])
         quantise(0, "q")

@@ -19,7 +19,7 @@ HEADS = 4
 N = 512
 SCALE = 1.0 / math.sqrt(N)
 FLOPS = 2 * 2 * HEADS * N * N * N
-V_SHARE = (N // RUN, 0, 0, 0)
+V_SHARE = (N // RUN, N // RUN // 2, 0, 0)
 
 
 def tile_model_kernel(tc, x1, query, key, value, out):
@@ -240,5 +240,7 @@ def tile_model_kernel(tc, x1, query, key, value, out):
                     mx_pass(p + 1, "k", "q", "st", "A", t)
             if p == 0:
                 regroup_v(0, "v")
+            if p + 1 < HEADS:
+                regroup_v(p + 1, "v")
             if 1 <= p <= HEADS:
                 finish(p - 1, PACK if p == HEADS else 1)

import math
from contextlib import ExitStack

import concourse.mybir as mybir
from concourse.masks import make_identity

F32 = mybir.dt.float32
BF16 = mybir.dt.bfloat16
U32 = mybir.dt.uint32
U8 = mybir.dt.uint8
FP8X4 = mybir.dt.float8_e4m3fn_x4
ACT = mybir.ActivationFunctionType
ALU = mybir.AluOpType

P = 128
PACK = 4
RUN = 4
HEADS = 4
N = 512
SCALE = 1.0 / math.sqrt(N)
FLOPS = 2 * 2 * HEADS * N * N * N
V_SHARE = (N // RUN, N // RUN // 2, 0, 0)


def tile_model_kernel(tc, x1, query, key, value, out):
    nc = tc.nc
    with ExitStack() as ctx:
        const = ctx.enter_context(tc.tile_pool(name="const", bufs=1))
        raw = ctx.enter_context(tc.tile_pool(name="raw", bufs=HEADS))
        vgrp = ctx.enter_context(tc.tile_pool(name="vgrp", bufs=HEADS))
        grp = ctx.enter_context(tc.tile_pool(name="grp", bufs=2))
        mxp = ctx.enter_context(tc.tile_pool(name="mxp", bufs=2))
        soft = ctx.enter_context(tc.tile_pool(name="soft", bufs=2))
        small = ctx.enter_context(tc.tile_pool(name="small", bufs=2))
        res = ctx.enter_context(tc.tile_pool(name="res", bufs=2))
        psum = ctx.enter_context(tc.psum_pool(name="psum", bufs=4))
        ctx.enter_context(tc.manual_schedule())

        def bank(name, half):
            return psum.tile([P, N], F32, name=name, tag=half)

        raws = {}

        def load(src, nm, h, pieces):
            t = raw.tile([P, PACK, N], BF16, name=nm, tag=nm)
            view = src[0, h].rearrange("(p j) d -> p j d", j=PACK)
            step = PACK // pieces
            for i in range(pieces):
                js = slice(step * i, step * i + step)
                nc.sync.dma_start(out=t[:, js, :], in_=view[:, js, :])
            raws[(nm, h)] = t

        for h in range(HEADS + 1):
            if h < HEADS:
                load(query, "q", h, 2 if h == 0 else 1)
                load(key, "k", h, 2 if h == 0 else 1)
            if h >= 1:
                load(value, "v", h - 1, 1)

        ident = const.tile([P, P], F32, name="ident")
        make_identity(nc, ident[:])
        warm_in = const.tile([P, 1], F32, name="warm_in")
        warm_out = const.tile([P, 1], F32, name="warm_out")
        nc.vector.memset(warm_in[:], 0.0)
        nc.scalar.activation(out=warm_out[:], in_=warm_in[:], func=ACT.Exp)

        zeros = const.tile([P, N], BF16, name="zeros")
        nc.vector.memset(zeros[:], 0.0)

        state = {}

        def copy(engine, dst, srcv):
            if engine == "s":
                nc.scalar.copy(out=dst, in_=srcv)
            else:
                nc.vector.tensor_copy(out=dst, in_=srcv)

        def transposes(h, half, warm=(0, 0, 0, 0)):
            banks = []
            for nm in ("q", "k"):
                words = raws[(nm, h)][:].rearrange("p j d -> p (j d)").bitcast(F32)
                for b in range(2):
                    tp = bank("t" + nm, half)
                    tpv = tp[:].rearrange("p (u r) -> p u r", u=2)
                    for w in range(warm[len(banks)]):
                        nc.tensor.matmul(out=tp[:], lhsT=zeros[:, 0:P], rhs=zeros[:], start=True, stop=True)
                    for jj in range(2):
                        for u in range(2):
                            c0 = (N // 2) * (2 * b + jj) + P * u
                            nc.tensor.transpose(tpv[:, u, P * jj : P * jj + P], words[:, c0 : c0 + P], ident[:])
                    banks.append(tpv)
            state[("tp", h)] = banks
            state[("qg", h)] = grp.tile([P, N * PACK], BF16, name="qg", tag="qg", align_bytes=64)
            state[("kg", h)] = grp.tile([P, N * PACK], BF16, name="kg", tag="kg", align_bytes=64)

        def gather(h, i, engine):
            xg = state[(("qg", "kg")[i // 2], h)]
            b = i % 2
            dst = xg[:].bitcast(F32)[:, N * b : N * b + N].rearrange("p (r u) -> p r u", u=2)
            copy(engine, dst, state[("tp", h)][i].rearrange("p u r -> p r u"))

        def mx_tiles(h, what):
            codes = mxp.tile([P, N], U32, name=what + "_codes", tag=what + "_codes", align_bytes=64)
            scales = mxp.tile([P, N], U8, name=what + "_scales", tag=what + "_scales", align_bytes=64)
            state[(what, h)] = (codes, scales)

        def quantise(h, what, lo=0, hi=N):
            if lo == 0:
                mx_tiles(h, what)
            codes, scales = state[(what, h)]
            nc.vector.quantize_mx(
                out=codes[:, lo:hi].bitcast(FP8X4),
                scales=scales[:, lo:hi],
                in_=state[(what + "g", h)][:, PACK * lo : PACK * hi],
            )

        def mx_pass(h, stat, mov, name, half, t):
            sc, ss = state[(stat, h)]
            mc, ms = state[(mov, h)]
            acc = bank(name, half)
            cols = slice(P * t, P * t + P)
            nc.tensor.matmul_mx(
                out=acc[:],
                lhsT=sc[:, cols].bitcast(FP8X4),
                lhsT_scale=ss[:, cols],
                rhs=mc[:].bitcast(FP8X4),
                rhs_scale=ms[:],
                start=True,
                stop=True,
            )
            state[(name, h, t)] = acc

        def reciprocal(h):
            r = small.tile([P, PACK], F32, name="r", tag="r")
            nc.vector.reciprocal(out=r[:], in_=state[("sums", h)][:])
            state[("r", h)] = r

        def softmax_exp(h, gathered):
            nb = small.tile([P, PACK], F32, name="nb", tag="nb")
            sums = small.tile([P, PACK], F32, name="sums", tag="sums")
            neg = soft.tile([P, PACK, N], F32, name="neg", tag="neg")
            e = soft.tile([P, PACK, N], F32, name="e", tag="e")
            state[("sums", h)] = sums
            state[("e", h)] = e
            for t in range(PACK):
                if t == PACK - 1 and h >= 1:
                    reciprocal(h - 1)
                nc.vector.tensor_scalar(
                    out=neg[:, t, :],
                    in0=state[("st", h, t)][:],
                    scalar1=-SCALE,
                    scalar2=None,
                    op0=ALU.mult,
                    op1=ALU.min,
                    accum_out=nb[:, t : t + 1],
                )
                nc.scalar.activation(
                    out=e[:, t, :],
                    in_=neg[:, t, :],
                    func=ACT.Exp,
                    bias=nb[:, t : t + 1],
                    scale=-1.0,
                    accum_out=sums[:, t : t + 1],
                )
                if gathered < HEADS:
                    gather(gathered, t, "s")

        def regroup_v(h, engine):
            if ("vg", h) not in state:
                state[("vg", h)] = vgrp.tile([P, N * PACK], BF16, name="vg", tag="vg", align_bytes=64)
            dst = state[("vg", h)][:].rearrange("p (c i t) -> p c t i", i=RUN, t=PACK)
            srcv = raws[("v", h)][:].rearrange("p t (c i) -> p c t i", i=RUN)
            cut = V_SHARE[h]
            if engine == "v" and cut > 0:
                copy("v", dst[:, 0:cut], srcv[:, 0:cut])
            if engine == "s" and cut < N // RUN:
                copy("s", dst[:, cut:], srcv[:, cut:])

        def normalise(h, lo, hi):
            if lo == 0:
                state[("pg", h)] = grp.tile([P, N * PACK], BF16, name="pg", tag="pg", align_bytes=64)
            pg = state[("pg", h)]
            nc.vector.tensor_tensor(
                out=pg[:, PACK * lo : PACK * hi].rearrange("p (c i t) -> p c t i", i=RUN, t=PACK),
                in0=state[("e", h)][:, :, lo:hi].rearrange("p t (c i) -> p c t i", i=RUN),
                in1=state[("r", h)][:].unsqueeze(1).unsqueeze(3).to_broadcast([P, (hi - lo) // RUN, PACK, RUN]),
                op=ALU.mult,
            )

        def finish(h, chunks):
            width = N // chunks
            for i in range(chunks + 1):
                if i < chunks:
                    normalise(h, width * i, width * i + width)
                if i == 0:
                    quantise(h, "v")
                    if h + 1 == HEADS - 1:
                        reciprocal(h + 1)
                if i >= 1:
                    quantise(h, "p", width * (i - 1), width * i)
                    for t in range(width * (i - 1) // P, width * i // P):
                        mx_pass(h, "p", "v", "ot", "B", t)

        def store(h, engines, per_store):
            o_sb = res.tile([P, PACK, N], F32, name="o_sb", tag="o_sb")
            view = out[0, h].rearrange("(p j) n -> p j n", j=PACK)
            for j in range(PACK):
                copy(engines[j], o_sb[:, j, :], state[("ot", h, j)][:])
                if (j + 1) % per_store == 0:
                    js = slice(j + 1 - per_store, j + 1)
                    nc.sync.dma_start(out=view[:, js, :], in_=o_sb[:, js, :])

        transposes(0, "A", (3, 1, 1, 1))
        transposes(1, "B", (1, 1, 1, 0))
        for i in range(4):
            gather(0, i, "sv"[i % 2])
        quantise(0, "q")
        quantise(0, "k")
        for t in range(PACK):
            mx_pass(0, "k", "q", "st", "A", t)
        for i in range(4):
            gather(1, i, "s")

        for p in range(HEADS + 2):
            if p + 2 < HEADS:
                transposes(p + 2, "B")
            if p + 1 < HEADS:
                quantise(p + 1, "q")
            if p < HEADS:
                softmax_exp(p, p + 2)
            if p >= 2:
                if p - 2 == HEADS - 1:
                    store(p - 2, "sssv", 1)
                else:
                    store(p - 2, "ssss", 2)
            if p + 1 < HEADS:
                regroup_v(p + 1, "s")
                quantise(p + 1, "k")
                for t in range(PACK):
                    mx_pass(p + 1, "k", "q", "st", "A", t)
            if p == 0:
                regroup_v(0, "v")
            if p + 1 < HEADS:
                regroup_v(p + 1, "v")
            if 1 <= p <= HEADS:
                finish(p - 1, PACK if p == HEADS else 1)
